import numpy as np
import ml_dtypes


def mxq(x, axis, fmt="e4m3"):
    dtype, down = {"e4m3": (ml_dtypes.float8_e4m3fn, 7), "e5m2": (ml_dtypes.float8_e5m2, 14)}[fmt]
    v = np.moveaxis(np.asarray(x, np.float32).astype(ml_dtypes.bfloat16).astype(np.float64), axis, -1)
    blocks = v.reshape(v.shape[:-1] + (-1, 32))
    amax = np.abs(blocks).max(-1, keepdims=True)
    byte = np.maximum(np.where(amax > 0, np.frexp(amax)[1] - 1 + 127, 0) - down, 1)
    scale = np.exp2(byte - 127.0)
    codes = (blocks / scale).astype(np.float32).astype(dtype).astype(np.float64)
    return np.moveaxis((codes * scale).reshape(v.shape), -1, axis)


WIDE = False


def mx_kscale(k):
    if not WIDE:
        return np.ones(k)
    levels = np.array([10, -10, 5, -5, 0])
    a = np.random.permutation(np.resize(levels, k // 512 * 4)).reshape(k // 512, 4)
    idx = np.arange(k)
    return np.exp2(a[idx // 512, idx % 128 // 32])


BF16 = ml_dtypes.bfloat16


def bf(x):
    return np.asarray(x, np.float32).astype(BF16)


def f64(x):
    return np.asarray(x).astype(np.float64)


B, N, E, H, C = 2, 2048, 256, 2, 512
D = E // H


def decay_gammas():
    return 1.0 - np.exp(np.linspace(np.log(2.0 ** -5), np.log(2.0 ** -9), H))


def setup_inputs():
    t = mx_kscale(N)
    return {"q_rot": bf(np.random.standard_normal((B, H, N, D))),
            "k_scaled": bf(np.random.standard_normal((B, H, N, D)) / np.sqrt(D) * t[:, None]),
            "v": bf(np.random.standard_normal((B, H, N, D)) * 0.5 / t[:, None])}


def reference(q_rot, k_scaled, v):
    q, k = f64(q_rot), f64(k_scaled)
    vq = mxq(f64(v), 2, "e4m3")
    gam = decay_gammas()[:, None, None]
    out = []
    for i in range(N // C):
        lo, hi = i * C, (i + 1) * C
        dist = f64(np.arange(lo, hi))[:, None] - f64(np.arange(hi))[None, :]
        mask = gam ** np.where(dist < 0, np.inf, dist)
        sim = (q[:, :, lo:hi] @ k[:, :, :hi].transpose(0, 1, 3, 2)) * mask[None]
        out.append(mxq(sim, 3, "e4m3") @ vq[:, :, :hi])
    ret = np.concatenate(out, axis=2)
    return ret.transpose(0, 2, 1, 3).reshape(B, N, E)

@@ -1,0 +1,203 @@
+import math
+from contextlib import ExitStack
+
+import concourse.mybir as mybir
+from concourse.masks import make_identity
+
+BF16 = mybir.dt.bfloat16
+F32 = mybir.dt.float32
+I32 = mybir.dt.int32
+U32 = mybir.dt.uint32
+U8 = mybir.dt.uint8
+FP8X4 = mybir.dt.float8_e4m3fn_x4
+
+P = 128
+PACK = 4
+CHUNK = P * PACK
+B, H, N, D = 2, 2, 2048, 128
+PAIRS = B * H
+CHUNKS = N // CHUNK
+TILES = N // P
+
+GAMMA = (1.0 - math.exp(math.log(2.0**-5)), 1.0 - math.exp(math.log(2.0**-9)))
+
+DIAGONAL = TILES - 1
+TABLE_TILES = DIAGONAL + PACK
+
+FLOPS = 2 * 2 * D * PAIRS * CHUNK * CHUNK * (CHUNKS * (CHUNKS + 1) // 2)
+
+
+def tile_multiscaleretention_pb_t_kernel(tc, q_rot, k_scaled, v, out):
+    nc = tc.nc
+    flat_inputs = {
+        "k": k_scaled.flatten_outer_dims(),
+        "q": q_rot.flatten_outer_dims(),
+        "v": v.flatten_outer_dims(),
+    }
+    out_flat = out.flatten_outer_dims()
+
+    with ExitStack() as ctx:
+        consts = ctx.enter_context(tc.tile_pool(name="consts", bufs=1))
+        inputs = ctx.enter_context(tc.tile_pool(name="inputs", bufs=1))
+        turned_pool = ctx.enter_context(tc.tile_pool(name="turned", bufs=2))
+        values_pool = ctx.enter_context(tc.tile_pool(name="values", bufs=2))
+        work = ctx.enter_context(tc.tile_pool(name="work", bufs=4))
+        results = ctx.enter_context(tc.tile_pool(name="results", bufs=2))
+        psum_turn = ctx.enter_context(tc.psum_pool(name="psum_turn", bufs=2))
+        psum_sim = ctx.enter_context(tc.psum_pool(name="psum_sim", bufs=3))
+        psum_acc = ctx.enter_context(tc.psum_pool(name="psum_acc", bufs=2))
+
+        rows = {}
+        for pair in range(PAIRS):
+            for chunk in range(CHUNKS):
+                first_row = pair * N + chunk * CHUNK
+                for which in ("k", "q", "v"):
+                    loaded = inputs.tile(
+                        [P, PACK, D], BF16, name="%s_rows_%d_%d" % (which, pair, chunk)
+                    )
+                    nc.sync.dma_start(
+                        out=loaded[:],
+                        in_=flat_inputs[which][first_row : first_row + CHUNK, :].rearrange(
+                            "(t p) d -> p t d", p=P
+                        ),
+                    )
+                    rows[(which, pair, chunk)] = loaded
+
+        identity = consts.tile([P, P], BF16)
+        make_identity(nc, identity[:])
+
+        distance_int = consts.tile([P, P], I32)
+        nc.gpsimd.iota(distance_int[:], pattern=[[1, P]], base=0, channel_multiplier=-1)
+        distance = consts.tile([P, P], F32)
+        nc.vector.tensor_copy(out=distance[:], in_=distance_int[:])
+        decay = []
+        for head in range(H):
+            near = consts.tile([P, P], F32, name="near_%d" % head)
+            nc.scalar.activation(
+                out=near[:],
+                in_=distance[:],
+                func=mybir.ActivationFunctionType.Exp,
+                scale=math.log(GAMMA[head]),
+            )
+            table = consts.tile([P, TABLE_TILES, P], F32, name="decay_%d" % head)
+            nc.gpsimd.memset(table[:, DIAGONAL + 1 :, :], 0.0)
+            nc.gpsimd.affine_select(
+                out=table[:, DIAGONAL, :],
+                in_=near[:],
+                pattern=[[1, P]],
+                compare_op=mybir.AluOpType.is_ge,
+                fill=0.0,
+                base=0,
+                channel_multiplier=-1,
+            )
+            for ahead in range(1, TILES):
+                nc.scalar.mul(
+                    out=table[:, DIAGONAL - ahead, :],
+                    in_=near[:],
+                    mul=GAMMA[head] ** (P * ahead),
+                )
+            decay.append(table)
+
+        def prepare(pair, chunk):
+            turned_ps = psum_turn.tile([P, 2 * PACK, P], BF16)
+            for t in range(PACK):
+                nc.tensor.transpose(
+                    turned_ps[:, t, :], rows[("k", pair, chunk)][:, t, :], identity[:]
+                )
+            for t in range(PACK):
+                nc.tensor.transpose(
+                    turned_ps[:, PACK + t, :], rows[("q", pair, chunk)][:, t, :], identity[:]
+                )
+            turned = turned_pool.tile([P, 2 * PACK, P], BF16, name="turned_%d" % chunk)
+            nc.scalar.copy(out=turned[:], in_=turned_ps[:])
+
+            v_grouped = work.tile([P, D, PACK], BF16, align_bytes=64)
+            nc.scalar.copy(
+                out=v_grouped[:], in_=rows[("v", pair, chunk)][:].rearrange("p t d -> p d t")
+            )
+            v_codes = values_pool.tile([P, D], U32, name="v_codes_%d" % chunk, align_bytes=64)
+            v_scales = values_pool.tile([P, D], U8, name="v_scales_%d" % chunk, align_bytes=64)
+            nc.vector.quantize_mx(
+                out=v_codes[:].bitcast(FP8X4),
+                scales=v_scales[:],
+                in_=v_grouped[:].rearrange("p d t -> p (d t)"),
+            )
+            return {"turned": turned, "v_codes": v_codes, "v_scales": v_scales}
+
+        def masked_products(keys, queries, slot, table, ahead):
+            sim_ps = psum_sim.tile([P, PACK, P], F32)
+            for t in range(PACK):
+                nc.tensor.matmul(
+                    out=sim_ps[:, t, :],
+                    lhsT=keys["turned"][:, t, :],
+                    rhs=queries["turned"][:, PACK + slot, :],
+                    start=True,
+                    stop=True,
+                )
+            first = DIAGONAL - ahead
+            grouped = work.tile([P, P, PACK], BF16, align_bytes=64)
+            nc.vector.tensor_tensor(
+                out=grouped[:],
+                in0=sim_ps[:].rearrange("p t w -> p w t"),
+                in1=table[:, first : first + PACK, :].rearrange("p t w -> p w t"),
+                op=mybir.AluOpType.mult,
+            )
+            return grouped
+
+        def contract(grouped, keys, acc_columns, start, stop):
+            codes = work.tile([P, P], U32, align_bytes=64)
+            scales = work.tile([P, P], U8, align_bytes=64)
+            nc.vector.quantize_mx(
+                out=codes[:].bitcast(FP8X4),
+                scales=scales[:],
+                in_=grouped[:].rearrange("p w t -> p (w t)"),
+            )
+            nc.tensor.matmul_mx(
+                out=acc_columns,
+                lhsT=codes[:].bitcast(FP8X4),
+                lhsT_scale=scales[:],
+                rhs=keys["v_codes"][:].bitcast(FP8X4),
+                rhs_scale=keys["v_scales"][:],
+                start=start,
+                stop=stop,
+            )
+
+        def store(acc, pair, chunk):
+            result = results.tile([P, PACK, D], F32)
+            nc.scalar.copy(out=result[:], in_=acc[:])
+            first_row = (pair // H) * N + chunk * CHUNK
+            first_column = (pair % H) * D
+            nc.sync.dma_start(
+                out=out_flat[
+                    first_row : first_row + CHUNK, first_column : first_column + D
+                ].rearrange("(t p) d -> p t d", p=P),
+                in_=result[:],
+            )
+
+        steps = []
+        for pair in range(PAIRS):
+            for chunk in range(CHUNKS):
+                steps.append((pair, chunk))
+
+        prepared = {steps[0]: prepare(*steps[0])}
+        waiting = None
+        finished = None
+        for index, (pair, chunk) in enumerate(steps):
+            if index + 1 < len(steps):
+                prepared[steps[index + 1]] = prepare(*steps[index + 1])
+            queries = prepared[(pair, chunk)]
+            acc = psum_acc.tile([P, PACK, D], F32)
+            for slot in range(PACK):
+                for key_chunk in range(chunk + 1):
+                    keys = prepared[(pair, key_chunk)]
+                    ahead = PACK * (chunk - key_chunk) + slot
+                    grouped = masked_products(keys, queries, slot, decay[pair % H], ahead)
+                    if waiting is not None:
+                        contract(*waiting)
+                    if finished is not None:
+                        store(*finished)
+                    waiting = (grouped, keys, acc[:, slot, :], key_chunk == 0, key_chunk == chunk)
+                    last_of_step = slot == PACK - 1 and key_chunk == chunk
+                    finished = (acc, pair, chunk) if last_of_step else None
+        contract(*waiting)
+        store(*finished)

@@ -24,6 +24,9 @@ GAMMA = (1.0 - math.exp(math.log(2.0**-5)), 1.0 - math.exp(math.log(2.0**-9)))
 DIAGONAL = TILES - 1
 TABLE_TILES = DIAGONAL + PACK
 
+GROUP = 8
+AHEAD = 2
+
 FLOPS = 2 * 2 * D * PAIRS * CHUNK * CHUNK * (CHUNKS * (CHUNKS + 1) // 2)
 
 
@@ -37,14 +40,15 @@ def tile_multiscaleretention_pb_t_kernel(tc, q_rot, k_scaled, v, out):
     out_flat = out.flatten_outer_dims()
 
     with ExitStack() as ctx:
+        ctx.enter_context(tc.manual_schedule())
         consts = ctx.enter_context(tc.tile_pool(name="consts", bufs=1))
         inputs = ctx.enter_context(tc.tile_pool(name="inputs", bufs=1))
         turned_pool = ctx.enter_context(tc.tile_pool(name="turned", bufs=2))
         values_pool = ctx.enter_context(tc.tile_pool(name="values", bufs=2))
-        work = ctx.enter_context(tc.tile_pool(name="work", bufs=4))
-        results = ctx.enter_context(tc.tile_pool(name="results", bufs=2))
+        work = ctx.enter_context(tc.tile_pool(name="work", bufs=2))
+        results = ctx.enter_context(tc.tile_pool(name="results", bufs=3))
         psum_turn = ctx.enter_context(tc.psum_pool(name="psum_turn", bufs=2))
-        psum_sim = ctx.enter_context(tc.psum_pool(name="psum_sim", bufs=3))
+        psum_sim = ctx.enter_context(tc.psum_pool(name="psum_sim", bufs=AHEAD + 1))
         psum_acc = ctx.enter_context(tc.psum_pool(name="psum_acc", bufs=2))
 
         rows = {}
@@ -63,11 +67,10 @@ def tile_multiscaleretention_pb_t_kernel(tc, q_rot, k_scaled, v, out):
                     )
                     rows[(which, pair, chunk)] = loaded
 
-        identity = consts.tile([P, P], BF16)
-        make_identity(nc, identity[:])
-
         distance_int = consts.tile([P, P], I32)
         nc.gpsimd.iota(distance_int[:], pattern=[[1, P]], base=0, channel_multiplier=-1)
+        identity = consts.tile([P, P], BF16)
+        make_identity(nc, identity[:])
         distance = consts.tile([P, P], F32)
         nc.vector.tensor_copy(out=distance[:], in_=distance_int[:])
         decay = []
@@ -91,14 +94,23 @@ def tile_multiscaleretention_pb_t_kernel(tc, q_rot, k_scaled, v, out):
                 channel_multiplier=-1,
             )
             for ahead in range(1, TILES):
-                nc.scalar.mul(
+                nc.vector.tensor_scalar_mul(
                     out=table[:, DIAGONAL - ahead, :],
-                    in_=near[:],
-                    mul=GAMMA[head] ** (P * ahead),
+                    in0=near[:],
+                    scalar1=GAMMA[head] ** (P * ahead),
                 )
             decay.append(table)
 
-        def prepare(pair, chunk):
+        turned = {}
+        v_grouped = {}
+        v_quantised = {}
+
+        def turn(pair, chunk):
+            values = work.tile([P, D, PACK], BF16, align_bytes=64)
+            nc.scalar.copy(
+                out=values[:], in_=rows[("v", pair, chunk)][:].rearrange("p t d -> p d t")
+            )
+            v_grouped[(pair, chunk)] = values
             turned_ps = psum_turn.tile([P, 2 * PACK, P], BF16)
             for t in range(PACK):
                 nc.tensor.transpose(
@@ -108,58 +120,39 @@ def tile_multiscaleretention_pb_t_kernel(tc, q_rot, k_scaled, v, out):
                 nc.tensor.transpose(
                     turned_ps[:, PACK + t, :], rows[("q", pair, chunk)][:, t, :], identity[:]
                 )
-            turned = turned_pool.tile([P, 2 * PACK, P], BF16, name="turned_%d" % chunk)
-            nc.scalar.copy(out=turned[:], in_=turned_ps[:])
+            kq = turned_pool.tile([P, 2 * PACK, P], BF16, name="turned_%d" % chunk)
+            nc.scalar.copy(out=kq[:], in_=turned_ps[:])
+            turned[(pair, chunk)] = kq
 
-            v_grouped = work.tile([P, D, PACK], BF16, align_bytes=64)
-            nc.scalar.copy(
-                out=v_grouped[:], in_=rows[("v", pair, chunk)][:].rearrange("p t d -> p d t")
-            )
+        def quantise_values(pair, chunk):
             v_codes = values_pool.tile([P, D], U32, name="v_codes_%d" % chunk, align_bytes=64)
             v_scales = values_pool.tile([P, D], U8, name="v_scales_%d" % chunk, align_bytes=64)
             nc.vector.quantize_mx(
                 out=v_codes[:].bitcast(FP8X4),
                 scales=v_scales[:],
-                in_=v_grouped[:].rearrange("p d t -> p (d t)"),
+                in_=v_grouped[(pair, chunk)][:].rearrange("p d t -> p (d t)"),
             )
-            return {"turned": turned, "v_codes": v_codes, "v_scales": v_scales}
+            v_quantised[(pair, chunk)] = (v_codes, v_scales)
 
-        def masked_products(keys, queries, slot, table, ahead):
+        def products(pair, chunk, slot, key_chunk):
             sim_ps = psum_sim.tile([P, PACK, P], F32)
             for t in range(PACK):
                 nc.tensor.matmul(
                     out=sim_ps[:, t, :],
-                    lhsT=keys["turned"][:, t, :],
-                    rhs=queries["turned"][:, PACK + slot, :],
+                    lhsT=turned[(pair, key_chunk)][:, t, :],
+                    rhs=turned[(pair, chunk)][:, PACK + slot, :],
                     start=True,
                     stop=True,
                 )
-            first = DIAGONAL - ahead
-            grouped = work.tile([P, P, PACK], BF16, align_bytes=64)
-            nc.vector.tensor_tensor(
-                out=grouped[:],
-                in0=sim_ps[:].rearrange("p t w -> p w t"),
-                in1=table[:, first : first + PACK, :].rearrange("p t w -> p w t"),
-                op=mybir.AluOpType.mult,
-            )
-            return grouped
+            return sim_ps
 
-        def contract(grouped, keys, acc_columns, start, stop):
-            codes = work.tile([P, P], U32, align_bytes=64)
-            scales = work.tile([P, P], U8, align_bytes=64)
-            nc.vector.quantize_mx(
-                out=codes[:].bitcast(FP8X4),
-                scales=scales[:],
-                in_=grouped[:].rearrange("p w t -> p (w t)"),
-            )
-            nc.tensor.matmul_mx(
-                out=acc_columns,
-                lhsT=codes[:].bitcast(FP8X4),
-                lhsT_scale=scales[:],
-                rhs=keys["v_codes"][:].bitcast(FP8X4),
-                rhs_scale=keys["v_scales"][:],
-                start=start,
-                stop=stop,
+        def mask(sim_ps, grouped_bank, pair, chunk, slot, key_chunk):
+            first = DIAGONAL - (PACK * (chunk - key_chunk) + slot)
+            nc.vector.tensor_tensor(
+                out=grouped_bank,
+                in0=sim_ps[:].rearrange("p t w -> p w t"),
+                in1=decay[pair % H][:, first : first + PACK, :].rearrange("p t w -> p w t"),
+                op=mybir.AluOpType.mult,
             )
 
         def store(acc, pair, chunk):
@@ -167,37 +160,68 @@ def tile_multiscaleretention_pb_t_kernel(tc, q_rot, k_scaled, v, out):
             nc.scalar.copy(out=result[:], in_=acc[:])
             first_row = (pair // H) * N + chunk * CHUNK
             first_column = (pair % H) * D
-            nc.sync.dma_start(
+            nc.scalar.dma_start(
                 out=out_flat[
                     first_row : first_row + CHUNK, first_column : first_column + D
                 ].rearrange("(t p) d -> p t d", p=P),
                 in_=result[:],
             )
 
-        steps = []
+        accs = {}
+
+        def contract(grouped, members):
+            codes = work.tile([P, GROUP, P], U32, align_bytes=64)
+            scales = work.tile([P, GROUP, P], U8, align_bytes=64)
+            nc.vector.quantize_mx(
+                out=codes[:].rearrange("p b w -> p (b w)").bitcast(FP8X4),
+                scales=scales[:].rearrange("p b w -> p (b w)"),
+                in_=grouped[:].rearrange("p b w t -> p (b w t)"),
+            )
+            for place, (pair, chunk, slot, key_chunk) in enumerate(members):
+                if slot == 0 and key_chunk == 0:
+                    acc = psum_acc.tile([P, PACK, D], F32)
+                    accs[(pair, chunk)] = acc
+                v_codes, v_scales = v_quantised[(pair, key_chunk)]
+                nc.tensor.matmul_mx(
+                    out=accs[(pair, chunk)][:, slot, :],
+                    lhsT=codes[:, place, :].bitcast(FP8X4),
+                    lhsT_scale=scales[:, place, :],
+                    rhs=v_codes[:].bitcast(FP8X4),
+                    rhs_scale=v_scales[:],
+                    start=(key_chunk == 0),
+                    stop=(key_chunk == chunk),
+                )
+                if slot == PACK - 1 and key_chunk == chunk:
+                    store(accs[(pair, chunk)], pair, chunk)
+
+        banks = []
         for pair in range(PAIRS):
             for chunk in range(CHUNKS):
-                steps.append((pair, chunk))
+                for slot in range(PACK):
+                    for key_chunk in range(chunk + 1):
+                        banks.append((pair, chunk, slot, key_chunk))
 
-        prepared = {steps[0]: prepare(*steps[0])}
-        waiting = None
-        finished = None
-        for index, (pair, chunk) in enumerate(steps):
-            if index + 1 < len(steps):
-                prepared[steps[index + 1]] = prepare(*steps[index + 1])
-            queries = prepared[(pair, chunk)]
-            acc = psum_acc.tile([P, PACK, D], F32)
-            for slot in range(PACK):
-                for key_chunk in range(chunk + 1):
-                    keys = prepared[(pair, key_chunk)]
-                    ahead = PACK * (chunk - key_chunk) + slot
-                    grouped = masked_products(keys, queries, slot, decay[pair % H], ahead)
-                    if waiting is not None:
-                        contract(*waiting)
-                    if finished is not None:
-                        store(*finished)
-                    waiting = (grouped, keys, acc[:, slot, :], key_chunk == 0, key_chunk == chunk)
-                    last_of_step = slot == PACK - 1 and key_chunk == chunk
-                    finished = (acc, pair, chunk) if last_of_step else None
-        contract(*waiting)
-        store(*finished)
+        turn(0, 0)
+        quantise_values(0, 0)
+        sim_banks = {}
+        grouped = None
+        for tick in range(len(banks) + AHEAD):
+            if tick < len(banks):
+                sim_banks[tick] = products(*banks[tick])
+            index = tick - AHEAD
+            if index < 0:
+                continue
+            pair, chunk, slot, key_chunk = banks[index]
+            full = grouped
+            if index % GROUP == 0:
+                grouped = work.tile([P, GROUP, P, PACK], BF16, align_bytes=64)
+            mask(sim_banks[index], grouped[:, index % GROUP, :, :], pair, chunk, slot, key_chunk)
+            following = pair * CHUNKS + chunk + 1
+            if following < PAIRS * CHUNKS:
+                if slot == 0 and key_chunk == 0:
+                    turn(following // CHUNKS, following % CHUNKS)
+                if slot == PACK - 1 and key_chunk == chunk:
+                    quantise_values(following // CHUNKS, following % CHUNKS)
+            if index % GROUP == 0 and index > 0:
+                contract(full, banks[index - GROUP : index])
+        contract(grouped, banks[len(banks) - GROUP :])

@@ -21,8 +21,7 @@ TILES = N // P
 
 GAMMA = (1.0 - math.exp(math.log(2.0**-5)), 1.0 - math.exp(math.log(2.0**-9)))
 
-DIAGONAL = TILES - 1
-TABLE_TILES = DIAGONAL + PACK
+FAR = PACK
 
 GROUP = 8
 AHEAD = 2
@@ -67,39 +66,40 @@ def tile_multiscaleretention_pb_t_kernel(tc, q_rot, k_scaled, v, out):
                     )
                     rows[(which, pair, chunk)] = loaded
 
-        distance_int = consts.tile([P, P], I32)
-        nc.gpsimd.iota(distance_int[:], pattern=[[1, P]], base=0, channel_multiplier=-1)
+        bank_pattern = [[1, P], [-P, PACK]]
+        distance_int = consts.tile([P, P, PACK], I32)
+        nc.gpsimd.iota(distance_int[:], pattern=bank_pattern, base=0, channel_multiplier=-1)
         identity = consts.tile([P, P], BF16)
         make_identity(nc, identity[:])
-        distance = consts.tile([P, P], F32)
+        distance = consts.tile([P, P, PACK], F32)
         nc.vector.tensor_copy(out=distance[:], in_=distance_int[:])
         decay = []
         for head in range(H):
-            near = consts.tile([P, P], F32, name="near_%d" % head)
+            near = consts.tile([P, P, PACK], F32, name="near_%d" % head)
             nc.scalar.activation(
                 out=near[:],
                 in_=distance[:],
                 func=mybir.ActivationFunctionType.Exp,
                 scale=math.log(GAMMA[head]),
             )
-            table = consts.tile([P, TABLE_TILES, P], F32, name="decay_%d" % head)
-            nc.gpsimd.memset(table[:, DIAGONAL + 1 :, :], 0.0)
-            nc.gpsimd.affine_select(
-                out=table[:, DIAGONAL, :],
-                in_=near[:],
-                pattern=[[1, P]],
-                compare_op=mybir.AluOpType.is_ge,
-                fill=0.0,
-                base=0,
-                channel_multiplier=-1,
-            )
-            for ahead in range(1, TILES):
+            head_masks = consts.tile([P, FAR + 1, P, PACK], F32, name="masks_%d" % head)
+            for ahead in range(FAR + 1):
                 nc.vector.tensor_scalar_mul(
-                    out=table[:, DIAGONAL - ahead, :],
+                    out=head_masks[:, ahead, :, :],
                     in0=near[:],
                     scalar1=GAMMA[head] ** (P * ahead),
                 )
-            decay.append(table)
+            for ahead in range(FAR):
+                nc.gpsimd.affine_select(
+                    out=head_masks[:, ahead, :, :],
+                    in_=head_masks[:, ahead, :, :],
+                    pattern=bank_pattern,
+                    compare_op=mybir.AluOpType.is_ge,
+                    fill=0.0,
+                    base=P * ahead,
+                    channel_multiplier=-1,
+                )
+            decay.append(head_masks)
 
         turned = {}
         v_grouped = {}
@@ -135,10 +135,10 @@ def tile_multiscaleretention_pb_t_kernel(tc, q_rot, k_scaled, v, out):
             v_quantised[(pair, chunk)] = (v_codes, v_scales)
 
         def products(pair, chunk, slot, key_chunk):
-            sim_ps = psum_sim.tile([P, PACK, P], F32)
+            sim_ps = psum_sim.tile([P, P, PACK], F32)
             for t in range(PACK):
                 nc.tensor.matmul(
-                    out=sim_ps[:, t, :],
+                    out=sim_ps[:, :, t],
                     lhsT=turned[(pair, key_chunk)][:, t, :],
                     rhs=turned[(pair, chunk)][:, PACK + slot, :],
                     start=True,
@@ -147,12 +147,15 @@ def tile_multiscaleretention_pb_t_kernel(tc, q_rot, k_scaled, v, out):
             return sim_ps
 
         def mask(sim_ps, grouped_bank, pair, chunk, slot, key_chunk):
-            first = DIAGONAL - (PACK * (chunk - key_chunk) + slot)
-            nc.vector.tensor_tensor(
+            ahead = PACK * (chunk - key_chunk) + slot
+            nearest = min(ahead, FAR)
+            nc.vector.scalar_tensor_tensor(
                 out=grouped_bank,
-                in0=sim_ps[:].rearrange("p t w -> p w t"),
-                in1=decay[pair % H][:, first : first + PACK, :].rearrange("p t w -> p w t"),
-                op=mybir.AluOpType.mult,
+                in0=sim_ps[:],
+                scalar=GAMMA[pair % H] ** (P * (ahead - nearest)),
+                in1=decay[pair % H][:, nearest, :, :],
+                op0=mybir.AluOpType.mult,
+                op1=mybir.AluOpType.mult,
             )
 
         def store(acc, pair, chunk):

@@ -24,7 +24,7 @@ GAMMA = (1.0 - math.exp(math.log(2.0**-5)), 1.0 - math.exp(math.log(2.0**-9)))
 FAR = PACK
 
 GROUP = 8
-AHEAD = 2
+AHEAD = 4
 
 FLOPS = 2 * 2 * D * PAIRS * CHUNK * CHUNK * (CHUNKS * (CHUNKS + 1) // 2)
 
@@ -46,7 +46,7 @@ def tile_multiscaleretention_pb_t_kernel(tc, q_rot, k_scaled, v, out):
         values_pool = ctx.enter_context(tc.tile_pool(name="values", bufs=2))
         work = ctx.enter_context(tc.tile_pool(name="work", bufs=2))
         results = ctx.enter_context(tc.tile_pool(name="results", bufs=3))
-        psum_turn = ctx.enter_context(tc.psum_pool(name="psum_turn", bufs=2))
+        psum_turn = ctx.enter_context(tc.psum_pool(name="psum_turn", bufs=1))
         psum_sim = ctx.enter_context(tc.psum_pool(name="psum_sim", bufs=AHEAD + 1))
         psum_acc = ctx.enter_context(tc.psum_pool(name="psum_acc", bufs=2))
 
@@ -211,6 +211,10 @@ def tile_multiscaleretention_pb_t_kernel(tc, q_rot, k_scaled, v, out):
         for tick in range(len(banks) + AHEAD):
             if tick < len(banks):
                 sim_banks[tick] = products(*banks[tick])
+                pair, chunk, slot, key_chunk = banks[tick]
+                following = pair * CHUNKS + chunk + 1
+                if slot == 0 and key_chunk == 0 and following < PAIRS * CHUNKS:
+                    turn(following // CHUNKS, following % CHUNKS)
             index = tick - AHEAD
             if index < 0:
                 continue
@@ -220,11 +224,8 @@ def tile_multiscaleretention_pb_t_kernel(tc, q_rot, k_scaled, v, out):
                 grouped = work.tile([P, GROUP, P, PACK], BF16, align_bytes=64)
             mask(sim_banks[index], grouped[:, index % GROUP, :, :], pair, chunk, slot, key_chunk)
             following = pair * CHUNKS + chunk + 1
-            if following < PAIRS * CHUNKS:
-                if slot == 0 and key_chunk == 0:
-                    turn(following // CHUNKS, following % CHUNKS)
-                if slot == PACK - 1 and key_chunk == chunk:
-                    quantise_values(following // CHUNKS, following % CHUNKS)
+            if slot == PACK - 1 and key_chunk == chunk and following < PAIRS * CHUNKS:
+                quantise_values(following // CHUNKS, following % CHUNKS)
             if index % GROUP == 0 and index > 0:
                 contract(full, banks[index - GROUP : index])
         contract(grouped, banks[len(banks) - GROUP :])

@@ -25,6 +25,7 @@ FAR = PACK
 
 GROUP = 8
 AHEAD = 4
+HELPED = 3
 
 FLOPS = 2 * 2 * D * PAIRS * CHUNK * CHUNK * (CHUNKS * (CHUNKS + 1) // 2)
 
@@ -45,6 +46,7 @@ def tile_multiscaleretention_pb_t_kernel(tc, q_rot, k_scaled, v, out):
         turned_pool = ctx.enter_context(tc.tile_pool(name="turned", bufs=2))
         values_pool = ctx.enter_context(tc.tile_pool(name="values", bufs=2))
         work = ctx.enter_context(tc.tile_pool(name="work", bufs=2))
+        handover = ctx.enter_context(tc.tile_pool(name="handover", bufs=4))
         results = ctx.enter_context(tc.tile_pool(name="results", bufs=3))
         psum_turn = ctx.enter_context(tc.psum_pool(name="psum_turn", bufs=1))
         psum_sim = ctx.enter_context(tc.psum_pool(name="psum_sim", bufs=AHEAD + 1))
@@ -158,6 +160,20 @@ def tile_multiscaleretention_pb_t_kernel(tc, q_rot, k_scaled, v, out):
                 op1=mybir.AluOpType.mult,
             )
 
+        def mask_with_helpers(sim_ps, grouped_bank, pair, chunk, slot, key_chunk):
+            ahead = PACK * (chunk - key_chunk) + slot
+            nearest = min(ahead, FAR)
+            scaled = handover.tile([P, P, PACK], F32)
+            nc.scalar.mul(
+                out=scaled[:], in_=sim_ps[:], mul=GAMMA[pair % H] ** (P * (ahead - nearest))
+            )
+            nc.gpsimd.tensor_tensor(
+                out=grouped_bank,
+                in0=scaled[:],
+                in1=decay[pair % H][:, nearest, :, :],
+                op=mybir.AluOpType.mult,
+            )
+
         def store(acc, pair, chunk):
             result = results.tile([P, PACK, D], F32)
             nc.scalar.copy(out=result[:], in_=acc[:])
@@ -207,10 +223,20 @@ def tile_multiscaleretention_pb_t_kernel(tc, q_rot, k_scaled, v, out):
         turn(0, 0)
         quantise_values(0, 0)
         sim_banks = {}
-        grouped = None
+        groups = {}
+        contracted = 0
         for tick in range(len(banks) + AHEAD):
             if tick < len(banks):
-                sim_banks[tick] = products(*banks[tick])
+                if tick % GROUP == 0:
+                    grouped = work.tile([P, GROUP, P, PACK], BF16, align_bytes=64)
+                    groups[tick // GROUP] = grouped
+                sim_ps = products(*banks[tick])
+                if tick % HELPED == HELPED - 1:
+                    mask_with_helpers(
+                        sim_ps, groups[tick // GROUP][:, tick % GROUP, :, :], *banks[tick]
+                    )
+                else:
+                    sim_banks[tick] = sim_ps
                 pair, chunk, slot, key_chunk = banks[tick]
                 following = pair * CHUNKS + chunk + 1
                 if slot == 0 and key_chunk == 0 and following < PAIRS * CHUNKS:
@@ -219,13 +245,13 @@ def tile_multiscaleretention_pb_t_kernel(tc, q_rot, k_scaled, v, out):
             if index < 0:
                 continue
             pair, chunk, slot, key_chunk = banks[index]
-            full = grouped
-            if index % GROUP == 0:
-                grouped = work.tile([P, GROUP, P, PACK], BF16, align_bytes=64)
-            mask(sim_banks[index], grouped[:, index % GROUP, :, :], pair, chunk, slot, key_chunk)
+            if index in sim_banks:
+                mask(sim_banks[index], groups[index // GROUP][:, index % GROUP, :, :], *banks[index])
+                if index // GROUP > contracted:
+                    first = contracted * GROUP
+                    contract(groups[contracted], banks[first : first + GROUP])
+                    contracted += 1
             following = pair * CHUNKS + chunk + 1
             if slot == PACK - 1 and key_chunk == chunk and following < PAIRS * CHUNKS:
                 quantise_values(following // CHUNKS, following % CHUNKS)
-            if index % GROUP == 0 and index > 0:
-                contract(full, banks[index - GROUP : index])
-        contract(grouped, banks[len(banks) - GROUP :])
+        contract(groups[contracted], banks[contracted * GROUP :])

@@ -6,7 +6,6 @@ from concourse.masks import make_identity
 
 BF16 = mybir.dt.bfloat16
 F32 = mybir.dt.float32
-I32 = mybir.dt.int32
 U32 = mybir.dt.uint32
 U8 = mybir.dt.uint8
 FP8X4 = mybir.dt.float8_e4m3fn_x4
@@ -17,15 +16,14 @@ CHUNK = P * PACK
 B, H, N, D = 2, 2, 2048, 128
 PAIRS = B * H
 CHUNKS = N // CHUNK
-TILES = N // P
 
 GAMMA = (1.0 - math.exp(math.log(2.0**-5)), 1.0 - math.exp(math.log(2.0**-9)))
 
 FAR = PACK
 
 GROUP = 8
-AHEAD = 4
-HELPED = 3
+COUPLE = 2
+LEAD = 2
 
 FLOPS = 2 * 2 * D * PAIRS * CHUNK * CHUNK * (CHUNKS * (CHUNKS + 1) // 2)
 
@@ -46,10 +44,8 @@ def tile_multiscaleretention_pb_t_kernel(tc, q_rot, k_scaled, v, out):
         turned_pool = ctx.enter_context(tc.tile_pool(name="turned", bufs=2))
         values_pool = ctx.enter_context(tc.tile_pool(name="values", bufs=2))
         work = ctx.enter_context(tc.tile_pool(name="work", bufs=2))
-        handover = ctx.enter_context(tc.tile_pool(name="handover", bufs=4))
         results = ctx.enter_context(tc.tile_pool(name="results", bufs=3))
-        psum_turn = ctx.enter_context(tc.psum_pool(name="psum_turn", bufs=1))
-        psum_sim = ctx.enter_context(tc.psum_pool(name="psum_sim", bufs=AHEAD + 1))
+        psum_sim = ctx.enter_context(tc.psum_pool(name="psum_sim", bufs=COUPLE * (LEAD + 1)))
         psum_acc = ctx.enter_context(tc.psum_pool(name="psum_acc", bufs=2))
 
         rows = {}
@@ -69,39 +65,47 @@ def tile_multiscaleretention_pb_t_kernel(tc, q_rot, k_scaled, v, out):
                     rows[(which, pair, chunk)] = loaded
 
         bank_pattern = [[1, P], [-P, PACK]]
-        distance_int = consts.tile([P, P, PACK], I32)
-        nc.gpsimd.iota(distance_int[:], pattern=bank_pattern, base=0, channel_multiplier=-1)
+        distance = consts.tile([P, P, PACK], F32)
+        nc.gpsimd.iota(
+            distance[:],
+            pattern=bank_pattern,
+            base=0,
+            channel_multiplier=-1,
+            allow_small_or_imprecise_dtypes=True,
+        )
         identity = consts.tile([P, P], BF16)
         make_identity(nc, identity[:])
-        distance = consts.tile([P, P, PACK], F32)
-        nc.vector.tensor_copy(out=distance[:], in_=distance_int[:])
+        near = []
         decay = []
         for head in range(H):
-            near = consts.tile([P, P, PACK], F32, name="near_%d" % head)
+            head_near = consts.tile([P, P, PACK], F32, name="near_%d" % head)
             nc.scalar.activation(
-                out=near[:],
+                out=head_near[:],
                 in_=distance[:],
                 func=mybir.ActivationFunctionType.Exp,
                 scale=math.log(GAMMA[head]),
             )
-            head_masks = consts.tile([P, FAR + 1, P, PACK], F32, name="masks_%d" % head)
-            for ahead in range(FAR + 1):
-                nc.vector.tensor_scalar_mul(
-                    out=head_masks[:, ahead, :, :],
-                    in0=near[:],
-                    scalar1=GAMMA[head] ** (P * ahead),
-                )
+            near.append(head_near)
+            head_decay = consts.tile([P, FAR + 1, P, PACK], F32, name="decay_%d" % head)
+            decay.append(head_decay)
+
+        def cut_off(head):
             for ahead in range(FAR):
                 nc.gpsimd.affine_select(
-                    out=head_masks[:, ahead, :, :],
-                    in_=head_masks[:, ahead, :, :],
+                    out=decay[head][:, ahead, :, :],
+                    in_=decay[head][:, ahead, :, :],
                     pattern=bank_pattern,
                     compare_op=mybir.AluOpType.is_ge,
                     fill=0.0,
                     base=P * ahead,
                     channel_multiplier=-1,
                 )
-            decay.append(head_masks)
+
+        for ahead in range(FAR + 1):
+            nc.vector.tensor_scalar_mul(
+                out=decay[0][:, ahead, :, :], in0=near[0][:], scalar1=GAMMA[0] ** (P * ahead)
+            )
+        cut_off(0)
 
         turned = {}
         v_grouped = {}
@@ -113,7 +117,7 @@ def tile_multiscaleretention_pb_t_kernel(tc, q_rot, k_scaled, v, out):
                 out=values[:], in_=rows[("v", pair, chunk)][:].rearrange("p t d -> p d t")
             )
             v_grouped[(pair, chunk)] = values
-            turned_ps = psum_turn.tile([P, 2 * PACK, P], BF16)
+            turned_ps = psum_sim.tile([P, 2 * PACK, P], BF16, tag="bank")
             for t in range(PACK):
                 nc.tensor.transpose(
                     turned_ps[:, t, :], rows[("k", pair, chunk)][:, t, :], identity[:]
@@ -137,7 +141,7 @@ def tile_multiscaleretention_pb_t_kernel(tc, q_rot, k_scaled, v, out):
             v_quantised[(pair, chunk)] = (v_codes, v_scales)
 
         def products(pair, chunk, slot, key_chunk):
-            sim_ps = psum_sim.tile([P, P, PACK], F32)
+            sim_ps = psum_sim.tile([P, P, PACK], F32, tag="bank")
             for t in range(PACK):
                 nc.tensor.matmul(
                     out=sim_ps[:, :, t],
@@ -158,20 +162,6 @@ def tile_multiscaleretention_pb_t_kernel(tc, q_rot, k_scaled, v, out):
                 in1=decay[pair % H][:, nearest, :, :],
                 op0=mybir.AluOpType.mult,
                 op1=mybir.AluOpType.mult,
-            )
-
-        def mask_with_helpers(sim_ps, grouped_bank, pair, chunk, slot, key_chunk):
-            ahead = PACK * (chunk - key_chunk) + slot
-            nearest = min(ahead, FAR)
-            scaled = handover.tile([P, P, PACK], F32)
-            nc.scalar.mul(
-                out=scaled[:], in_=sim_ps[:], mul=GAMMA[pair % H] ** (P * (ahead - nearest))
-            )
-            nc.gpsimd.tensor_tensor(
-                out=grouped_bank,
-                in0=scaled[:],
-                in1=decay[pair % H][:, nearest, :, :],
-                op=mybir.AluOpType.mult,
             )
 
         def store(acc, pair, chunk):
@@ -222,36 +212,37 @@ def tile_multiscaleretention_pb_t_kernel(tc, q_rot, k_scaled, v, out):
 
         turn(0, 0)
         quantise_values(0, 0)
+
         sim_banks = {}
-        groups = {}
-        contracted = 0
-        for tick in range(len(banks) + AHEAD):
-            if tick < len(banks):
-                if tick % GROUP == 0:
-                    grouped = work.tile([P, GROUP, P, PACK], BF16, align_bytes=64)
-                    groups[tick // GROUP] = grouped
-                sim_ps = products(*banks[tick])
-                if tick % HELPED == HELPED - 1:
-                    mask_with_helpers(
-                        sim_ps, groups[tick // GROUP][:, tick % GROUP, :, :], *banks[tick]
-                    )
-                else:
-                    sim_banks[tick] = sim_ps
-                pair, chunk, slot, key_chunk = banks[tick]
-                following = pair * CHUNKS + chunk + 1
-                if slot == 0 and key_chunk == 0 and following < PAIRS * CHUNKS:
-                    turn(following // CHUNKS, following % CHUNKS)
-            index = tick - AHEAD
-            if index < 0:
+        grouped = None
+        couples = len(banks) // COUPLE
+        for beat in range(-LEAD, couples):
+            filled = beat + LEAD
+            if filled < couples:
+                for index in range(COUPLE * filled, COUPLE * (filled + 1)):
+                    sim_banks[index] = products(*banks[index])
+                    pair, chunk, slot, key_chunk = banks[index]
+                    following = pair * CHUNKS + chunk + 1
+                    if slot == 0 and key_chunk == 0 and following < PAIRS * CHUNKS:
+                        turn(following // CHUNKS, following % CHUNKS)
+            if beat < 0:
                 continue
-            pair, chunk, slot, key_chunk = banks[index]
-            if index in sim_banks:
-                mask(sim_banks[index], groups[index // GROUP][:, index % GROUP, :, :], *banks[index])
-                if index // GROUP > contracted:
-                    first = contracted * GROUP
-                    contract(groups[contracted], banks[first : first + GROUP])
-                    contracted += 1
+            if beat == 0:
+                for ahead in range(FAR + 1):
+                    nc.scalar.mul(
+                        out=decay[1][:, ahead, :, :], in_=near[1][:], mul=GAMMA[1] ** (P * ahead)
+                    )
+                cut_off(1)
+            first = COUPLE * beat
+            full = grouped
+            if first % GROUP == 0:
+                grouped = work.tile([P, GROUP, P, PACK], BF16, align_bytes=64)
+            for index in reversed(range(first, first + COUPLE)):
+                mask(sim_banks[index], grouped[:, index % GROUP, :, :], *banks[index])
+            pair, chunk, slot, key_chunk = banks[first + COUPLE - 1]
             following = pair * CHUNKS + chunk + 1
             if slot == PACK - 1 and key_chunk == chunk and following < PAIRS * CHUNKS:
                 quantise_values(following // CHUNKS, following % CHUNKS)
-        contract(groups[contracted], banks[contracted * GROUP :])
+            if first % GROUP == 0 and first > 0:
+                contract(full, banks[first - GROUP : first])
+        contract(grouped, banks[len(banks) - GROUP :])

import math
from contextlib import ExitStack

import concourse.mybir as mybir
from concourse.masks import make_identity

BF16 = mybir.dt.bfloat16
F32 = mybir.dt.float32
U32 = mybir.dt.uint32
U8 = mybir.dt.uint8
FP8X4 = mybir.dt.float8_e4m3fn_x4

P = 128
PACK = 4
CHUNK = P * PACK
B, H, N, D = 2, 2, 2048, 128
PAIRS = B * H
CHUNKS = N // CHUNK

GAMMA = (1.0 - math.exp(math.log(2.0**-5)), 1.0 - math.exp(math.log(2.0**-9)))

FAR = PACK

GROUP = 8
COUPLE = 2
LEAD = 2

FLOPS = 2 * 2 * D * PAIRS * CHUNK * CHUNK * (CHUNKS * (CHUNKS + 1) // 2)


def tile_multiscaleretention_pb_t_kernel(tc, q_rot, k_scaled, v, out):
    nc = tc.nc
    flat_inputs = {
        "k": k_scaled.flatten_outer_dims(),
        "q": q_rot.flatten_outer_dims(),
        "v": v.flatten_outer_dims(),
    }
    out_flat = out.flatten_outer_dims()

    with ExitStack() as ctx:
        ctx.enter_context(tc.manual_schedule())
        consts = ctx.enter_context(tc.tile_pool(name="consts", bufs=1))
        inputs = ctx.enter_context(tc.tile_pool(name="inputs", bufs=1))
        turned_pool = ctx.enter_context(tc.tile_pool(name="turned", bufs=2))
        values_pool = ctx.enter_context(tc.tile_pool(name="values", bufs=2))
        work = ctx.enter_context(tc.tile_pool(name="work", bufs=2))
        results = ctx.enter_context(tc.tile_pool(name="results", bufs=3))
        psum_sim = ctx.enter_context(tc.psum_pool(name="psum_sim", bufs=COUPLE * (LEAD + 1)))
        psum_acc = ctx.enter_context(tc.psum_pool(name="psum_acc", bufs=2))

        rows = {}
        for pair in range(PAIRS):
            for chunk in range(CHUNKS):
                first_row = pair * N + chunk * CHUNK
                for which in ("k", "q", "v"):
                    loaded = inputs.tile(
                        [P, PACK, D], BF16, name="%s_rows_%d_%d" % (which, pair, chunk)
                    )
                    nc.sync.dma_start(
                        out=loaded[:],
                        in_=flat_inputs[which][first_row : first_row + CHUNK, :].rearrange(
                            "(t p) d -> p t d", p=P
                        ),
                    )
                    rows[(which, pair, chunk)] = loaded

        bank_pattern = [[1, P], [-P, PACK]]
        distance = consts.tile([P, P, PACK], F32)
        nc.gpsimd.iota(
            distance[:],
            pattern=bank_pattern,
            base=0,
            channel_multiplier=-1,
            allow_small_or_imprecise_dtypes=True,
        )
        identity = consts.tile([P, P], BF16)
        make_identity(nc, identity[:])
        near = []
        decay = []
        for head in range(H):
            head_near = consts.tile([P, P, PACK], F32, name="near_%d" % head)
            nc.scalar.activation(
                out=head_near[:],
                in_=distance[:],
                func=mybir.ActivationFunctionType.Exp,
                scale=math.log(GAMMA[head]),
            )
            near.append(head_near)
            head_decay = consts.tile([P, FAR + 1, P, PACK], F32, name="decay_%d" % head)
            decay.append(head_decay)

        def cut_off(head):
            for ahead in range(FAR):
                nc.gpsimd.affine_select(
                    out=decay[head][:, ahead, :, :],
                    in_=decay[head][:, ahead, :, :],
                    pattern=bank_pattern,
                    compare_op=mybir.AluOpType.is_ge,
                    fill=0.0,
                    base=P * ahead,
                    channel_multiplier=-1,
                )

        for ahead in range(FAR + 1):
            nc.vector.tensor_scalar_mul(
                out=decay[0][:, ahead, :, :], in0=near[0][:], scalar1=GAMMA[0] ** (P * ahead)
            )
        cut_off(0)

        turned = {}
        v_grouped = {}
        v_quantised = {}

        def turn(pair, chunk):
            values = work.tile([P, D, PACK], BF16, align_bytes=64)
            nc.scalar.copy(
                out=values[:], in_=rows[("v", pair, chunk)][:].rearrange("p t d -> p d t")
            )
            v_grouped[(pair, chunk)] = values
            turned_ps = psum_sim.tile([P, 2 * PACK, P], BF16, tag="bank")
            for t in range(PACK):
                nc.tensor.transpose(
                    turned_ps[:, t, :], rows[("k", pair, chunk)][:, t, :], identity[:]
                )
            for t in range(PACK):
                nc.tensor.transpose(
                    turned_ps[:, PACK + t, :], rows[("q", pair, chunk)][:, t, :], identity[:]
                )
            kq = turned_pool.tile([P, 2 * PACK, P], BF16, name="turned_%d" % chunk)
            nc.scalar.copy(out=kq[:], in_=turned_ps[:])
            turned[(pair, chunk)] = kq

        def quantise_values(pair, chunk):
            v_codes = values_pool.tile([P, D], U32, name="v_codes_%d" % chunk, align_bytes=64)
            v_scales = values_pool.tile([P, D], U8, name="v_scales_%d" % chunk, align_bytes=64)
            nc.vector.quantize_mx(
                out=v_codes[:].bitcast(FP8X4),
                scales=v_scales[:],
                in_=v_grouped[(pair, chunk)][:].rearrange("p d t -> p (d t)"),
            )
            v_quantised[(pair, chunk)] = (v_codes, v_scales)

        def products(pair, chunk, slot, key_chunk):
            sim_ps = psum_sim.tile([P, P, PACK], F32, tag="bank")
            for t in range(PACK):
                nc.tensor.matmul(
                    out=sim_ps[:, :, t],
                    lhsT=turned[(pair, key_chunk)][:, t, :],
                    rhs=turned[(pair, chunk)][:, PACK + slot, :],
                    start=True,
                    stop=True,
                )
            return sim_ps

        def mask(sim_ps, grouped_bank, pair, chunk, slot, key_chunk):
            ahead = PACK * (chunk - key_chunk) + slot
            nearest = min(ahead, FAR)
            nc.vector.scalar_tensor_tensor(
                out=grouped_bank,
                in0=sim_ps[:],
                scalar=GAMMA[pair % H] ** (P * (ahead - nearest)),
                in1=decay[pair % H][:, nearest, :, :],
                op0=mybir.AluOpType.mult,
                op1=mybir.AluOpType.mult,
            )

        def store(acc, pair, chunk):
            result = results.tile([P, PACK, D], F32)
            nc.scalar.copy(out=result[:], in_=acc[:])
            first_row = (pair // H) * N + chunk * CHUNK
            first_column = (pair % H) * D
            nc.scalar.dma_start(
                out=out_flat[
                    first_row : first_row + CHUNK, first_column : first_column + D
                ].rearrange("(t p) d -> p t d", p=P),
                in_=result[:],
            )

        accs = {}

        def contract(grouped, members):
            codes = work.tile([P, GROUP, P], U32, align_bytes=64)
            scales = work.tile([P, GROUP, P], U8, align_bytes=64)
            nc.vector.quantize_mx(
                out=codes[:].rearrange("p b w -> p (b w)").bitcast(FP8X4),
                scales=scales[:].rearrange("p b w -> p (b w)"),
                in_=grouped[:].rearrange("p b w t -> p (b w t)"),
            )
            for place, (pair, chunk, slot, key_chunk) in enumerate(members):
                if slot == 0 and key_chunk == 0:
                    acc = psum_acc.tile([P, PACK, D], F32)
                    accs[(pair, chunk)] = acc
                v_codes, v_scales = v_quantised[(pair, key_chunk)]
                nc.tensor.matmul_mx(
                    out=accs[(pair, chunk)][:, slot, :],
                    lhsT=codes[:, place, :].bitcast(FP8X4),
                    lhsT_scale=scales[:, place, :],
                    rhs=v_codes[:].bitcast(FP8X4),
                    rhs_scale=v_scales[:],
                    start=(key_chunk == 0),
                    stop=(key_chunk == chunk),
                )
                if slot == PACK - 1 and key_chunk == chunk:
                    store(accs[(pair, chunk)], pair, chunk)

        banks = []
        for pair in range(PAIRS):
            for chunk in range(CHUNKS):
                for slot in range(PACK):
                    for key_chunk in range(chunk + 1):
                        banks.append((pair, chunk, slot, key_chunk))

        turn(0, 0)
        quantise_values(0, 0)

        sim_banks = {}
        grouped = None
        couples = len(banks) // COUPLE
        for beat in range(-LEAD, couples):
            filled = beat + LEAD
            if filled < couples:
                for index in range(COUPLE * filled, COUPLE * (filled + 1)):
                    sim_banks[index] = products(*banks[index])
                    pair, chunk, slot, key_chunk = banks[index]
                    following = pair * CHUNKS + chunk + 1
                    if slot == 0 and key_chunk == 0 and following < PAIRS * CHUNKS:
                        turn(following // CHUNKS, following % CHUNKS)
            if beat < 0:
                continue
            if beat == 0:
                for ahead in range(FAR + 1):
                    nc.scalar.mul(
                        out=decay[1][:, ahead, :, :], in_=near[1][:], mul=GAMMA[1] ** (P * ahead)
                    )
                cut_off(1)
            first = COUPLE * beat
            full = grouped
            if first % GROUP == 0:
                grouped = work.tile([P, GROUP, P, PACK], BF16, align_bytes=64)
            for index in reversed(range(first, first + COUPLE)):
                mask(sim_banks[index], grouped[:, index % GROUP, :, :], *banks[index])
            pair, chunk, slot, key_chunk = banks[first + COUPLE - 1]
            following = pair * CHUNKS + chunk + 1
            if slot == PACK - 1 and key_chunk == chunk and following < PAIRS * CHUNKS:
                quantise_values(following // CHUNKS, following % CHUNKS)
            if first % GROUP == 0 and first > 0:
                contract(full, banks[first - GROUP : first])
        contract(grouped, banks[len(banks) - GROUP :])
